import numpy as np
import ml_dtypes

BF16 = ml_dtypes.bfloat16


def bf(x):
    return np.asarray(x, np.float32).astype(BF16)


def f32(x):
    return np.asarray(x, np.float32)


def f64(x):
    return np.asarray(x).astype(np.float64)


def striped(idx):
    return np.tile(idx.reshape(-1, 16).T, (8, 1))


A, S, N = 128, 1024, 1024
RATIO = 0.5
COUNT = 1.0
WT = 1.0 / (1.0 + COUNT)


def setup_inputs():
    return {
        "w": f32(2.0 * np.random.standard_normal((A, S)) / np.sqrt(A)),
        "cov_s": f32(np.abs(np.random.standard_normal((A, N)))),
        "mean_s": f32(np.random.standard_normal((A, N))),
        "feat": f32(np.random.standard_normal((A, N))),
        "y": f32(np.random.standard_normal((S, N))),
        "offs": striped(np.random.permutation(S)[:N]),
    }


def reference(w, cov_s, mean_s, feat, y, offs):
    idx = offs[:16].T.reshape(-1)
    w = f64(w)
    covn = (1.0 - WT) * f64(cov_s) + WT * (1.0 - WT) * (f64(mean_s) - f64(feat)) ** 2
    p = w[:, idx] * covn
    q = w[:, idx] * p
    t1 = (w * w).T @ covn
    t2 = w.T @ p
    t3 = q.sum(axis=0, keepdims=True)
    return f64(y) + 0.5 * RATIO * (t1 - 2.0 * t2 + t3)

@@ -1,0 +1,79 @@
+import concourse.mybir as mybir
+
+F32 = mybir.dt.float32
+BF16 = mybir.dt.bfloat16
+U16 = mybir.dt.uint16
+ADD = mybir.AluOpType.add
+SUBTRACT = mybir.AluOpType.subtract
+MULT = mybir.AluOpType.mult
+COPY = mybir.ActivationFunctionType.Copy
+SQUARE = mybir.ActivationFunctionType.Square
+
+A = 128
+S = 1024
+N = 1024
+BLOCK = 128
+BANK = 512
+
+FLOPS = 2 * A * S * N * 2 + 2 * A * N
+
+
+def tile_isdahead_kernel(tc, w, cov_s, mean_s, feat, y, offs, out):
+    nc = tc.nc
+    with (
+        tc.tile_pool(name="held", bufs=1) as held,
+        tc.tile_pool(name="logits", bufs=S // BLOCK) as logits,
+        tc.psum_pool(name="banks", bufs=8) as banks,
+    ):
+        offsets = held.tile([A, N // 16], U16, name="offsets")
+        nc.sync.dma_start(offsets[:], offs)
+        mean_t = held.tile([A, N], F32)
+        nc.sync.dma_start(mean_t[:], mean_s)
+        feat_t = held.tile([A, N], F32)
+        nc.scalar.dma_start(feat_t[:], feat)
+        cov_t = held.tile([A, N], F32)
+        nc.sync.dma_start(cov_t[:], cov_s)
+        w_t = held.tile([A, S], F32)
+        nc.scalar.dma_start(w_t[:], w)
+        y_blocks = []
+        for c in range(S // BLOCK):
+            y_t = logits.tile([BLOCK, N], F32)
+            nc.sync.dma_start(y_t[:], y[c * BLOCK : (c + 1) * BLOCK, :])
+            y_blocks.append(y_t)
+
+        quarter = held.tile([A, BLOCK], BF16)
+        nc.vector.memset(quarter[:], 0.25)
+        w_sq_quarter = held.tile([A, S], BF16)
+        nc.scalar.activation(w_sq_quarter[:], w_t[:], SQUARE, scale=0.5)
+        w_neg_half = held.tile([A, S], BF16)
+        nc.scalar.activation(w_neg_half[:], w_t[:], COPY, scale=-0.5)
+
+        diff = held.tile([A, N], F32)
+        nc.vector.tensor_tensor(diff[:], mean_t[:], feat_t[:], SUBTRACT)
+        diff_sq = held.tile([A, N], F32)
+        nc.scalar.activation(diff_sq[:], diff[:], SQUARE, scale=0.5)
+        covn = held.tile([A, N], F32)
+        nc.vector.scalar_tensor_tensor(covn[:], cov_t[:], 0.5, diff_sq[:], MULT, ADD)
+        covn_bf = held.tile([A, N], BF16)
+        nc.scalar.copy(covn_bf[:], covn[:])
+
+        p = held.tile([A, N], F32)
+        nc.vector.tensor_tensor(p[:], w_t[:].indirect(offsets[:]), covn[:], MULT)
+        p_bf = held.tile([A, N], BF16)
+        nc.scalar.copy(p_bf[:], p[:])
+        q = held.tile([A, N], F32)
+        nc.vector.tensor_tensor(q[:], w_t[:].indirect(offsets[:]), p[:], MULT)
+        q_bf = held.tile([A, N], BF16)
+        nc.scalar.copy(q_bf[:], q[:])
+
+        for c in range(S // BLOCK):
+            classes = slice(c * BLOCK, (c + 1) * BLOCK)
+            res = logits.tile([BLOCK, N], F32)
+            for h in range(N // BANK):
+                samples = slice(h * BANK, (h + 1) * BANK)
+                acc = banks.tile([BLOCK, BANK], F32)
+                nc.tensor.matmul(acc[:], w_sq_quarter[:, classes], covn_bf[:, samples], start=True, stop=False)
+                nc.tensor.matmul(acc[:], w_neg_half[:, classes], p_bf[:, samples], start=False, stop=False)
+                nc.tensor.matmul(acc[:], quarter[:], q_bf[:, samples], start=False, stop=True)
+                nc.vector.tensor_tensor(res[:, samples], acc[:], y_blocks[c][:, samples], ADD)
+            nc.sync.dma_start(out[classes, :], res[:])

@@ -20,6 +20,7 @@ FLOPS = 2 * A * S * N * 2 + 2 * A * N
 
 def tile_isdahead_kernel(tc, w, cov_s, mean_s, feat, y, offs, out):
     nc = tc.nc
+    halves = [slice(h * BANK, (h + 1) * BANK) for h in range(N // BANK)]
     with (
         tc.tile_pool(name="held", bufs=1) as held,
         tc.tile_pool(name="logits", bufs=S // BLOCK) as logits,
@@ -28,13 +29,16 @@ def tile_isdahead_kernel(tc, w, cov_s, mean_s, feat, y, offs, out):
         offsets = held.tile([A, N // 16], U16, name="offsets")
         nc.sync.dma_start(offsets[:], offs)
         mean_t = held.tile([A, N], F32)
-        nc.sync.dma_start(mean_t[:], mean_s)
         feat_t = held.tile([A, N], F32)
-        nc.scalar.dma_start(feat_t[:], feat)
         cov_t = held.tile([A, N], F32)
-        nc.sync.dma_start(cov_t[:], cov_s)
         w_t = held.tile([A, S], F32)
+        nc.sync.dma_start(mean_t[:, halves[0]], mean_s[:, halves[0]])
+        nc.scalar.dma_start(feat_t[:, halves[0]], feat[:, halves[0]])
+        nc.sync.dma_start(cov_t[:, halves[0]], cov_s[:, halves[0]])
         nc.scalar.dma_start(w_t[:], w)
+        nc.sync.dma_start(mean_t[:, halves[1]], mean_s[:, halves[1]])
+        nc.scalar.dma_start(feat_t[:, halves[1]], feat[:, halves[1]])
+        nc.sync.dma_start(cov_t[:, halves[1]], cov_s[:, halves[1]])
         y_blocks = []
         for c in range(S // BLOCK):
             y_t = logits.tile([BLOCK, N], F32)
@@ -42,35 +46,37 @@ def tile_isdahead_kernel(tc, w, cov_s, mean_s, feat, y, offs, out):
             y_blocks.append(y_t)
 
         quarter = held.tile([A, BLOCK], BF16)
-        nc.vector.memset(quarter[:], 0.25)
         w_sq_quarter = held.tile([A, S], BF16)
-        nc.scalar.activation(w_sq_quarter[:], w_t[:], SQUARE, scale=0.5)
         w_neg_half = held.tile([A, S], BF16)
-        nc.scalar.activation(w_neg_half[:], w_t[:], COPY, scale=-0.5)
+        nc.vector.memset(quarter[:], 0.25)
 
         diff = held.tile([A, N], F32)
-        nc.vector.tensor_tensor(diff[:], mean_t[:], feat_t[:], SUBTRACT)
         diff_sq = held.tile([A, N], F32)
-        nc.scalar.activation(diff_sq[:], diff[:], SQUARE, scale=0.5)
         covn = held.tile([A, N], F32)
-        nc.vector.scalar_tensor_tensor(covn[:], cov_t[:], 0.5, diff_sq[:], MULT, ADD)
-        covn_bf = held.tile([A, N], BF16)
-        nc.scalar.copy(covn_bf[:], covn[:])
-
         p = held.tile([A, N], F32)
-        nc.vector.tensor_tensor(p[:], w_t[:].indirect(offsets[:]), covn[:], MULT)
-        p_bf = held.tile([A, N], BF16)
-        nc.scalar.copy(p_bf[:], p[:])
         q = held.tile([A, N], F32)
-        nc.vector.tensor_tensor(q[:], w_t[:].indirect(offsets[:]), p[:], MULT)
+        covn_bf = held.tile([A, N], BF16)
+        p_bf = held.tile([A, N], BF16)
         q_bf = held.tile([A, N], BF16)
-        nc.scalar.copy(q_bf[:], q[:])
+        for h, samples in enumerate(halves):
+            piece = offsets[:, h * (BANK // 16) : (h + 1) * (BANK // 16)]
+            nc.vector.tensor_tensor(diff[:, samples], mean_t[:, samples], feat_t[:, samples], SUBTRACT)
+            nc.scalar.activation(diff_sq[:, samples], diff[:, samples], SQUARE, scale=0.5)
+            if h == 0:
+                nc.scalar.activation(w_sq_quarter[:], w_t[:], SQUARE, scale=0.5)
+            nc.vector.scalar_tensor_tensor(covn[:, samples], cov_t[:, samples], 0.5, diff_sq[:, samples], MULT, ADD)
+            nc.scalar.copy(covn_bf[:, samples], covn[:, samples])
+            if h == 0:
+                nc.scalar.activation(w_neg_half[:], w_t[:], COPY, scale=-0.5)
+            nc.vector.tensor_tensor(p[:, samples], w_t[:].indirect(piece), covn[:, samples], MULT)
+            nc.scalar.copy(p_bf[:, samples], p[:, samples])
+            nc.vector.tensor_tensor(q[:, samples], w_t[:].indirect(piece), p[:, samples], MULT)
+            nc.scalar.copy(q_bf[:, samples], q[:, samples])
 
         for c in range(S // BLOCK):
             classes = slice(c * BLOCK, (c + 1) * BLOCK)
             res = logits.tile([BLOCK, N], F32)
-            for h in range(N // BANK):
-                samples = slice(h * BANK, (h + 1) * BANK)
+            for samples in halves:
                 acc = banks.tile([BLOCK, BANK], F32)
                 nc.tensor.matmul(acc[:], w_sq_quarter[:, classes], covn_bf[:, samples], start=True, stop=False)
                 nc.tensor.matmul(acc[:], w_neg_half[:, classes], p_bf[:, samples], start=False, stop=False)

@@ -14,16 +14,19 @@ S = 1024
 N = 1024
 BLOCK = 128
 BANK = 512
+QUAD = 4
 
 FLOPS = 2 * A * S * N * 2 + 2 * A * N
 
 
 def tile_isdahead_kernel(tc, w, cov_s, mean_s, feat, y, offs, out):
     nc = tc.nc
+    n_blocks = S // BLOCK
     halves = [slice(h * BANK, (h + 1) * BANK) for h in range(N // BANK)]
     with (
         tc.tile_pool(name="held", bufs=1) as held,
-        tc.tile_pool(name="logits", bufs=S // BLOCK) as logits,
+        tc.tile_pool(name="logits", bufs=len(halves) * n_blocks // QUAD) as logits,
+        tc.tile_pool(name="results", bufs=len(halves) * n_blocks) as results,
         tc.psum_pool(name="banks", bufs=8) as banks,
     ):
         offsets = held.tile([A, N // 16], U16, name="offsets")
@@ -39,11 +42,13 @@ def tile_isdahead_kernel(tc, w, cov_s, mean_s, feat, y, offs, out):
         nc.sync.dma_start(mean_t[:, halves[1]], mean_s[:, halves[1]])
         nc.scalar.dma_start(feat_t[:, halves[1]], feat[:, halves[1]])
         nc.sync.dma_start(cov_t[:, halves[1]], cov_s[:, halves[1]])
-        y_blocks = []
-        for c in range(S // BLOCK):
-            y_t = logits.tile([BLOCK, N], F32)
-            nc.sync.dma_start(y_t[:], y[c * BLOCK : (c + 1) * BLOCK, :])
-            y_blocks.append(y_t)
+        y_by_block = y.rearrange("(c k) j -> k c j", k=BLOCK)
+        y_quads = []
+        for samples in halves:
+            for g in range(n_blocks // QUAD):
+                y_quad = logits.tile([BLOCK, QUAD, BANK], F32)
+                nc.sync.dma_start(y_quad[:], y_by_block[:, g * QUAD : (g + 1) * QUAD, samples])
+                y_quads.append(y_quad)
 
         quarter = held.tile([A, BLOCK], BF16)
         w_sq_quarter = held.tile([A, S], BF16)
@@ -73,13 +78,13 @@ def tile_isdahead_kernel(tc, w, cov_s, mean_s, feat, y, offs, out):
             nc.vector.tensor_tensor(q[:, samples], w_t[:].indirect(piece), p[:, samples], MULT)
             nc.scalar.copy(q_bf[:, samples], q[:, samples])
 
-        for c in range(S // BLOCK):
-            classes = slice(c * BLOCK, (c + 1) * BLOCK)
-            res = logits.tile([BLOCK, N], F32)
-            for samples in halves:
+            for c in range(n_blocks):
+                classes = slice(c * BLOCK, (c + 1) * BLOCK)
+                y_piece = y_quads[h * (n_blocks // QUAD) + c // QUAD][:, c % QUAD, :]
                 acc = banks.tile([BLOCK, BANK], F32)
                 nc.tensor.matmul(acc[:], w_sq_quarter[:, classes], covn_bf[:, samples], start=True, stop=False)
                 nc.tensor.matmul(acc[:], w_neg_half[:, classes], p_bf[:, samples], start=False, stop=False)
                 nc.tensor.matmul(acc[:], quarter[:], q_bf[:, samples], start=False, stop=True)
-                nc.vector.tensor_tensor(res[:, samples], acc[:], y_blocks[c][:, samples], ADD)
-            nc.sync.dma_start(out[classes, :], res[:])
+                res = results.tile([BLOCK, BANK], F32)
+                nc.vector.tensor_tensor(res[:], acc[:], y_piece, ADD)
+                nc.sync.dma_start(out[classes, samples], res[:])

@@ -15,6 +15,7 @@ N = 1024
 BLOCK = 128
 BANK = 512
 QUAD = 4
+WARM_UP = 9
 
 FLOPS = 2 * A * S * N * 2 + 2 * A * N
 
@@ -37,8 +38,8 @@ def tile_isdahead_kernel(tc, w, cov_s, mean_s, feat, y, offs, out):
         w_t = held.tile([A, S], F32)
         nc.sync.dma_start(mean_t[:, halves[0]], mean_s[:, halves[0]])
         nc.scalar.dma_start(feat_t[:, halves[0]], feat[:, halves[0]])
-        nc.sync.dma_start(cov_t[:, halves[0]], cov_s[:, halves[0]])
-        nc.scalar.dma_start(w_t[:], w)
+        nc.sync.dma_start(w_t[:], w)
+        nc.scalar.dma_start(cov_t[:, halves[0]], cov_s[:, halves[0]])
         nc.sync.dma_start(mean_t[:, halves[1]], mean_s[:, halves[1]])
         nc.scalar.dma_start(feat_t[:, halves[1]], feat[:, halves[1]])
         nc.sync.dma_start(cov_t[:, halves[1]], cov_s[:, halves[1]])
@@ -53,7 +54,13 @@ def tile_isdahead_kernel(tc, w, cov_s, mean_s, feat, y, offs, out):
         quarter = held.tile([A, BLOCK], BF16)
         w_sq_quarter = held.tile([A, S], BF16)
         w_neg_half = held.tile([A, S], BF16)
-        nc.vector.memset(quarter[:], 0.25)
+
+        half = held.tile([A, BANK], BF16)
+        nc.vector.memset(half[:], 0.5)
+        nc.scalar.activation(quarter[:], half[:, :BLOCK], SQUARE)
+        unused = banks.tile([BLOCK, BANK], F32, tag="acc")
+        for i in range(WARM_UP):
+            nc.tensor.matmul(unused[:], half[:, :BLOCK], half[:], start=True, stop=True)
 
         diff = held.tile([A, N], F32)
         diff_sq = held.tile([A, N], F32)
@@ -67,17 +74,17 @@ def tile_isdahead_kernel(tc, w, cov_s, mean_s, feat, y, offs, out):
             piece = offsets[:, h * (BANK // 16) : (h + 1) * (BANK // 16)]
             nc.vector.tensor_tensor(diff[:, samples], mean_t[:, samples], feat_t[:, samples], SUBTRACT)
             nc.scalar.activation(diff_sq[:, samples], diff[:, samples], SQUARE, scale=0.5)
+            nc.vector.scalar_tensor_tensor(covn[:, samples], cov_t[:, samples], 0.5, diff_sq[:, samples], MULT, ADD)
+            nc.vector.tensor_copy(covn_bf[:, samples], covn[:, samples])
             if h == 0:
                 nc.scalar.activation(w_sq_quarter[:], w_t[:], SQUARE, scale=0.5)
-            nc.vector.scalar_tensor_tensor(covn[:, samples], cov_t[:, samples], 0.5, diff_sq[:, samples], MULT, ADD)
-            nc.scalar.copy(covn_bf[:, samples], covn[:, samples])
-            if h == 0:
                 nc.scalar.activation(w_neg_half[:], w_t[:], COPY, scale=-0.5)
             nc.vector.tensor_tensor(p[:, samples], w_t[:].indirect(piece), covn[:, samples], MULT)
             nc.scalar.copy(p_bf[:, samples], p[:, samples])
             nc.vector.tensor_tensor(q[:, samples], w_t[:].indirect(piece), p[:, samples], MULT)
             nc.scalar.copy(q_bf[:, samples], q[:, samples])
 
+        for h, samples in enumerate(halves):
             for c in range(n_blocks):
                 classes = slice(c * BLOCK, (c + 1) * BLOCK)
                 y_piece = y_quads[h * (n_blocks // QUAD) + c // QUAD][:, c % QUAD, :]

@@ -14,7 +14,7 @@ S = 1024
 N = 1024
 BLOCK = 128
 BANK = 512
-QUAD = 4
+PAIR = 2
 WARM_UP = 9
 
 FLOPS = 2 * A * S * N * 2 + 2 * A * N
@@ -26,8 +26,8 @@ def tile_isdahead_kernel(tc, w, cov_s, mean_s, feat, y, offs, out):
     halves = [slice(h * BANK, (h + 1) * BANK) for h in range(N // BANK)]
     with (
         tc.tile_pool(name="held", bufs=1) as held,
-        tc.tile_pool(name="logits", bufs=len(halves) * n_blocks // QUAD) as logits,
-        tc.tile_pool(name="results", bufs=len(halves) * n_blocks) as results,
+        tc.tile_pool(name="logits", bufs=n_blocks // PAIR) as logits,
+        tc.tile_pool(name="results", bufs=n_blocks) as results,
         tc.psum_pool(name="banks", bufs=8) as banks,
     ):
         offsets = held.tile([A, N // 16], U16, name="offsets")
@@ -44,12 +44,11 @@ def tile_isdahead_kernel(tc, w, cov_s, mean_s, feat, y, offs, out):
         nc.scalar.dma_start(feat_t[:, halves[1]], feat[:, halves[1]])
         nc.sync.dma_start(cov_t[:, halves[1]], cov_s[:, halves[1]])
         y_by_block = y.rearrange("(c k) j -> k c j", k=BLOCK)
-        y_quads = []
-        for samples in halves:
-            for g in range(n_blocks // QUAD):
-                y_quad = logits.tile([BLOCK, QUAD, BANK], F32)
-                nc.sync.dma_start(y_quad[:], y_by_block[:, g * QUAD : (g + 1) * QUAD, samples])
-                y_quads.append(y_quad)
+        y_pairs = []
+        for g in range(n_blocks // PAIR):
+            y_pair = logits.tile([BLOCK, PAIR, N], F32)
+            nc.sync.dma_start(y_pair[:], y_by_block[:, g * PAIR : (g + 1) * PAIR, :])
+            y_pairs.append(y_pair)
 
         quarter = held.tile([A, BLOCK], BF16)
         w_sq_quarter = held.tile([A, S], BF16)
@@ -84,14 +83,14 @@ def tile_isdahead_kernel(tc, w, cov_s, mean_s, feat, y, offs, out):
             nc.vector.tensor_tensor(q[:, samples], w_t[:].indirect(piece), p[:, samples], MULT)
             nc.scalar.copy(q_bf[:, samples], q[:, samples])
 
+        res_blocks = [results.tile([BLOCK, N], F32, name="res") for c in range(n_blocks)]
         for h, samples in enumerate(halves):
             for c in range(n_blocks):
                 classes = slice(c * BLOCK, (c + 1) * BLOCK)
-                y_piece = y_quads[h * (n_blocks // QUAD) + c // QUAD][:, c % QUAD, :]
                 acc = banks.tile([BLOCK, BANK], F32)
                 nc.tensor.matmul(acc[:], w_sq_quarter[:, classes], covn_bf[:, samples], start=True, stop=False)
                 nc.tensor.matmul(acc[:], w_neg_half[:, classes], p_bf[:, samples], start=False, stop=False)
                 nc.tensor.matmul(acc[:], quarter[:], q_bf[:, samples], start=False, stop=True)
-                res = results.tile([BLOCK, BANK], F32)
-                nc.vector.tensor_tensor(res[:], acc[:], y_piece, ADD)
-                nc.sync.dma_start(out[classes, samples], res[:])
+                nc.vector.tensor_tensor(res_blocks[c][:, samples], acc[:], y_pairs[c // PAIR][:, c % PAIR, samples], ADD)
+                if h == len(halves) - 1:
+                    nc.sync.dma_start(out[classes, :], res_blocks[c][:])

@@ -14,8 +14,8 @@ S = 1024
 N = 1024
 BLOCK = 128
 BANK = 512
-PAIR = 2
-WARM_UP = 9
+QUAD = 4
+WARM_UP = 16
 
 FLOPS = 2 * A * S * N * 2 + 2 * A * N
 
@@ -26,8 +26,8 @@ def tile_isdahead_kernel(tc, w, cov_s, mean_s, feat, y, offs, out):
     halves = [slice(h * BANK, (h + 1) * BANK) for h in range(N // BANK)]
     with (
         tc.tile_pool(name="held", bufs=1) as held,
-        tc.tile_pool(name="logits", bufs=n_blocks // PAIR) as logits,
-        tc.tile_pool(name="results", bufs=n_blocks) as results,
+        tc.tile_pool(name="logits", bufs=len(halves) * n_blocks // QUAD) as logits,
+        tc.tile_pool(name="results", bufs=len(halves) * n_blocks) as results,
         tc.psum_pool(name="banks", bufs=8) as banks,
     ):
         offsets = held.tile([A, N // 16], U16, name="offsets")
@@ -36,19 +36,19 @@ def tile_isdahead_kernel(tc, w, cov_s, mean_s, feat, y, offs, out):
         feat_t = held.tile([A, N], F32)
         cov_t = held.tile([A, N], F32)
         w_t = held.tile([A, S], F32)
-        nc.sync.dma_start(mean_t[:, halves[0]], mean_s[:, halves[0]])
-        nc.scalar.dma_start(feat_t[:, halves[0]], feat[:, halves[0]])
+        for samples in halves:
+            nc.sync.dma_start(mean_t[:, samples], mean_s[:, samples])
+            nc.sync.dma_start(feat_t[:, samples], feat[:, samples])
+        nc.sync.dma_start(cov_t[:, halves[0]], cov_s[:, halves[0]])
         nc.sync.dma_start(w_t[:], w)
-        nc.scalar.dma_start(cov_t[:, halves[0]], cov_s[:, halves[0]])
-        nc.sync.dma_start(mean_t[:, halves[1]], mean_s[:, halves[1]])
-        nc.scalar.dma_start(feat_t[:, halves[1]], feat[:, halves[1]])
         nc.sync.dma_start(cov_t[:, halves[1]], cov_s[:, halves[1]])
         y_by_block = y.rearrange("(c k) j -> k c j", k=BLOCK)
-        y_pairs = []
-        for g in range(n_blocks // PAIR):
-            y_pair = logits.tile([BLOCK, PAIR, N], F32)
-            nc.sync.dma_start(y_pair[:], y_by_block[:, g * PAIR : (g + 1) * PAIR, :])
-            y_pairs.append(y_pair)
+        y_quads = []
+        for samples in halves:
+            for g in range(n_blocks // QUAD):
+                y_quad = logits.tile([BLOCK, QUAD, BANK], F32)
+                nc.sync.dma_start(y_quad[:], y_by_block[:, g * QUAD : (g + 1) * QUAD, samples])
+                y_quads.append(y_quad)
 
         quarter = held.tile([A, BLOCK], BF16)
         w_sq_quarter = held.tile([A, S], BF16)
@@ -83,14 +83,14 @@ def tile_isdahead_kernel(tc, w, cov_s, mean_s, feat, y, offs, out):
             nc.vector.tensor_tensor(q[:, samples], w_t[:].indirect(piece), p[:, samples], MULT)
             nc.scalar.copy(q_bf[:, samples], q[:, samples])
 
-        res_blocks = [results.tile([BLOCK, N], F32, name="res") for c in range(n_blocks)]
         for h, samples in enumerate(halves):
             for c in range(n_blocks):
                 classes = slice(c * BLOCK, (c + 1) * BLOCK)
+                y_piece = y_quads[h * (n_blocks // QUAD) + c // QUAD][:, c % QUAD, :]
                 acc = banks.tile([BLOCK, BANK], F32)
                 nc.tensor.matmul(acc[:], w_sq_quarter[:, classes], covn_bf[:, samples], start=True, stop=False)
                 nc.tensor.matmul(acc[:], w_neg_half[:, classes], p_bf[:, samples], start=False, stop=False)
                 nc.tensor.matmul(acc[:], quarter[:], q_bf[:, samples], start=False, stop=True)
-                nc.vector.tensor_tensor(res_blocks[c][:, samples], acc[:], y_pairs[c // PAIR][:, c % PAIR, samples], ADD)
-                if h == len(halves) - 1:
-                    nc.sync.dma_start(out[classes, :], res_blocks[c][:])
+                res = results.tile([BLOCK, BANK], F32)
+                nc.vector.tensor_tensor(res[:], acc[:], y_piece, ADD)
+                nc.sync.dma_start(out[classes, samples], res[:])

@@ -15,7 +15,7 @@ N = 1024
 BLOCK = 128
 BANK = 512
 QUAD = 4
-WARM_UP = 16
+WARM_UP = 9
 
 FLOPS = 2 * A * S * N * 2 + 2 * A * N
 
@@ -36,12 +36,12 @@ def tile_isdahead_kernel(tc, w, cov_s, mean_s, feat, y, offs, out):
         feat_t = held.tile([A, N], F32)
         cov_t = held.tile([A, N], F32)
         w_t = held.tile([A, S], F32)
-        for samples in halves:
+        for h, samples in enumerate(halves):
             nc.sync.dma_start(mean_t[:, samples], mean_s[:, samples])
             nc.sync.dma_start(feat_t[:, samples], feat[:, samples])
-        nc.sync.dma_start(cov_t[:, halves[0]], cov_s[:, halves[0]])
-        nc.sync.dma_start(w_t[:], w)
-        nc.sync.dma_start(cov_t[:, halves[1]], cov_s[:, halves[1]])
+            nc.sync.dma_start(cov_t[:, samples], cov_s[:, samples])
+            if h == 0:
+                nc.sync.dma_start(w_t[:], w)
         y_by_block = y.rearrange("(c k) j -> k c j", k=BLOCK)
         y_quads = []
         for samples in halves:

@@ -36,12 +36,12 @@ def tile_isdahead_kernel(tc, w, cov_s, mean_s, feat, y, offs, out):
         feat_t = held.tile([A, N], F32)
         cov_t = held.tile([A, N], F32)
         w_t = held.tile([A, S], F32)
-        for h, samples in enumerate(halves):
+        for samples in halves:
             nc.sync.dma_start(mean_t[:, samples], mean_s[:, samples])
             nc.sync.dma_start(feat_t[:, samples], feat[:, samples])
-            nc.sync.dma_start(cov_t[:, samples], cov_s[:, samples])
-            if h == 0:
-                nc.sync.dma_start(w_t[:], w)
+        nc.sync.dma_start(cov_t[:, halves[0]], cov_s[:, halves[0]])
+        nc.sync.dma_start(w_t[:], w)
+        nc.sync.dma_start(cov_t[:, halves[1]], cov_s[:, halves[1]])
         y_by_block = y.rearrange("(c k) j -> k c j", k=BLOCK)
         y_quads = []
         for samples in halves:

@@ -36,12 +36,12 @@ def tile_isdahead_kernel(tc, w, cov_s, mean_s, feat, y, offs, out):
         feat_t = held.tile([A, N], F32)
         cov_t = held.tile([A, N], F32)
         w_t = held.tile([A, S], F32)
-        for samples in halves:
+        for h, samples in enumerate(halves):
             nc.sync.dma_start(mean_t[:, samples], mean_s[:, samples])
             nc.sync.dma_start(feat_t[:, samples], feat[:, samples])
-        nc.sync.dma_start(cov_t[:, halves[0]], cov_s[:, halves[0]])
-        nc.sync.dma_start(w_t[:], w)
-        nc.sync.dma_start(cov_t[:, halves[1]], cov_s[:, halves[1]])
+            if h == 0:
+                nc.sync.dma_start(w_t[:], w)
+            nc.sync.dma_start(cov_t[:, samples], cov_s[:, samples])
         y_by_block = y.rearrange("(c k) j -> k c j", k=BLOCK)
         y_quads = []
         for samples in halves:
@@ -69,19 +69,36 @@ def tile_isdahead_kernel(tc, w, cov_s, mean_s, feat, y, offs, out):
         covn_bf = held.tile([A, N], BF16)
         p_bf = held.tile([A, N], BF16)
         q_bf = held.tile([A, N], BF16)
-        for h, samples in enumerate(halves):
-            piece = offsets[:, h * (BANK // 16) : (h + 1) * (BANK // 16)]
+
+        def squared_difference(h):
+            samples = halves[h]
             nc.vector.tensor_tensor(diff[:, samples], mean_t[:, samples], feat_t[:, samples], SUBTRACT)
             nc.scalar.activation(diff_sq[:, samples], diff[:, samples], SQUARE, scale=0.5)
+
+        def covariance(h):
+            samples = halves[h]
             nc.vector.scalar_tensor_tensor(covn[:, samples], cov_t[:, samples], 0.5, diff_sq[:, samples], MULT, ADD)
-            nc.vector.tensor_copy(covn_bf[:, samples], covn[:, samples])
             if h == 0:
-                nc.scalar.activation(w_sq_quarter[:], w_t[:], SQUARE, scale=0.5)
-                nc.scalar.activation(w_neg_half[:], w_t[:], COPY, scale=-0.5)
-            nc.vector.tensor_tensor(p[:, samples], w_t[:].indirect(piece), covn[:, samples], MULT)
-            nc.scalar.copy(p_bf[:, samples], p[:, samples])
-            nc.vector.tensor_tensor(q[:, samples], w_t[:].indirect(piece), p[:, samples], MULT)
-            nc.scalar.copy(q_bf[:, samples], q[:, samples])
+                nc.vector.tensor_copy(covn_bf[:, samples], covn[:, samples])
+            else:
+                nc.scalar.copy(covn_bf[:, samples], covn[:, samples])
+
+        def looked_up_product(h, product, product_bf, factor):
+            samples = halves[h]
+            piece = offsets[:, h * (BANK // 16) : (h + 1) * (BANK // 16)]
+            nc.vector.tensor_tensor(product[:, samples], w_t[:].indirect(piece), factor[:, samples], MULT)
+            nc.scalar.copy(product_bf[:, samples], product[:, samples])
+
+        squared_difference(0)
+        nc.scalar.activation(w_sq_quarter[:], w_t[:], SQUARE, scale=0.5)
+        covariance(0)
+        nc.scalar.activation(w_neg_half[:], w_t[:], COPY, scale=-0.5)
+        looked_up_product(0, p, p_bf, covn)
+        squared_difference(1)
+        looked_up_product(0, q, q_bf, p)
+        covariance(1)
+        looked_up_product(1, p, p_bf, covn)
+        looked_up_product(1, q, q_bf, p)
 
         for h, samples in enumerate(halves):
             for c in range(n_blocks):

@@ -15,6 +15,7 @@ N = 1024
 BLOCK = 128
 BANK = 512
 QUAD = 4
+PAIR = 2
 WARM_UP = 9
 
 FLOPS = 2 * A * S * N * 2 + 2 * A * N
@@ -27,7 +28,7 @@ def tile_isdahead_kernel(tc, w, cov_s, mean_s, feat, y, offs, out):
     with (
         tc.tile_pool(name="held", bufs=1) as held,
         tc.tile_pool(name="logits", bufs=len(halves) * n_blocks // QUAD) as logits,
-        tc.tile_pool(name="results", bufs=len(halves) * n_blocks) as results,
+        tc.tile_pool(name="results", bufs=len(halves) * n_blocks // PAIR) as results,
         tc.psum_pool(name="banks", bufs=8) as banks,
     ):
         offsets = held.tile([A, N // 16], U16, name="offsets")
@@ -43,6 +44,7 @@ def tile_isdahead_kernel(tc, w, cov_s, mean_s, feat, y, offs, out):
                 nc.sync.dma_start(w_t[:], w)
             nc.sync.dma_start(cov_t[:, samples], cov_s[:, samples])
         y_by_block = y.rearrange("(c k) j -> k c j", k=BLOCK)
+        out_by_block = out.rearrange("(c k) j -> k c j", k=BLOCK)
         y_quads = []
         for samples in halves:
             for g in range(n_blocks // QUAD):
@@ -108,6 +110,8 @@ def tile_isdahead_kernel(tc, w, cov_s, mean_s, feat, y, offs, out):
                 nc.tensor.matmul(acc[:], w_sq_quarter[:, classes], covn_bf[:, samples], start=True, stop=False)
                 nc.tensor.matmul(acc[:], w_neg_half[:, classes], p_bf[:, samples], start=False, stop=False)
                 nc.tensor.matmul(acc[:], quarter[:], q_bf[:, samples], start=False, stop=True)
-                res = results.tile([BLOCK, BANK], F32)
-                nc.vector.tensor_tensor(res[:], acc[:], y_piece, ADD)
-                nc.sync.dma_start(out[classes, samples], res[:])
+                if c % PAIR == 0:
+                    res = results.tile([BLOCK, PAIR, BANK], F32, name="res")
+                nc.vector.tensor_tensor(res[:, c % PAIR, :], acc[:], y_piece, ADD)
+                if c % PAIR == PAIR - 1:
+                    nc.sync.dma_start(out_by_block[:, c + 1 - PAIR : c + 1, samples], res[:])

@@ -25,6 +25,7 @@ def tile_isdahead_kernel(tc, w, cov_s, mean_s, feat, y, offs, out):
     nc = tc.nc
     n_blocks = S // BLOCK
     halves = [slice(h * BANK, (h + 1) * BANK) for h in range(N // BANK)]
+    class_halves = [slice(0, S // 2), slice(S // 2, S)]
     with (
         tc.tile_pool(name="held", bufs=1) as held,
         tc.tile_pool(name="logits", bufs=len(halves) * n_blocks // QUAD) as logits,
@@ -40,9 +41,9 @@ def tile_isdahead_kernel(tc, w, cov_s, mean_s, feat, y, offs, out):
         for h, samples in enumerate(halves):
             nc.sync.dma_start(mean_t[:, samples], mean_s[:, samples])
             nc.sync.dma_start(feat_t[:, samples], feat[:, samples])
+            nc.sync.dma_start(cov_t[:, samples], cov_s[:, samples])
             if h == 0:
                 nc.sync.dma_start(w_t[:], w)
-            nc.sync.dma_start(cov_t[:, samples], cov_s[:, samples])
         y_by_block = y.rearrange("(c k) j -> k c j", k=BLOCK)
         out_by_block = out.rearrange("(c k) j -> k c j", k=BLOCK)
         y_quads = []
@@ -92,11 +93,13 @@ def tile_isdahead_kernel(tc, w, cov_s, mean_s, feat, y, offs, out):
             nc.scalar.copy(product_bf[:, samples], product[:, samples])
 
         squared_difference(0)
-        nc.scalar.activation(w_sq_quarter[:], w_t[:], SQUARE, scale=0.5)
         covariance(0)
-        nc.scalar.activation(w_neg_half[:], w_t[:], COPY, scale=-0.5)
+        nc.scalar.activation(w_sq_quarter[:, class_halves[0]], w_t[:, class_halves[0]], SQUARE, scale=0.5)
+        nc.scalar.activation(w_sq_quarter[:, class_halves[1]], w_t[:, class_halves[1]], SQUARE, scale=0.5)
+        nc.scalar.activation(w_neg_half[:, class_halves[0]], w_t[:, class_halves[0]], COPY, scale=-0.5)
         looked_up_product(0, p, p_bf, covn)
         squared_difference(1)
+        nc.scalar.activation(w_neg_half[:, class_halves[1]], w_t[:, class_halves[1]], COPY, scale=-0.5)
         looked_up_product(0, q, q_bf, p)
         covariance(1)
         looked_up_product(1, p, p_bf, covn)

@@ -16,7 +16,6 @@ BLOCK = 128
 BANK = 512
 QUAD = 4
 PAIR = 2
-WARM_UP = 9
 
 FLOPS = 2 * A * S * N * 2 + 2 * A * N
 
@@ -57,12 +56,9 @@ def tile_isdahead_kernel(tc, w, cov_s, mean_s, feat, y, offs, out):
         w_sq_quarter = held.tile([A, S], BF16)
         w_neg_half = held.tile([A, S], BF16)
 
-        half = held.tile([A, BANK], BF16)
+        half = held.tile([A, BLOCK], BF16)
         nc.vector.memset(half[:], 0.5)
-        nc.scalar.activation(quarter[:], half[:, :BLOCK], SQUARE)
-        unused = banks.tile([BLOCK, BANK], F32, tag="acc")
-        for i in range(WARM_UP):
-            nc.tensor.matmul(unused[:], half[:, :BLOCK], half[:], start=True, stop=True)
+        nc.scalar.activation(quarter[:], half[:], SQUARE)
 
         diff = held.tile([A, N], F32)
         diff_sq = held.tile([A, N], F32)

@@ -14,7 +14,6 @@ S = 1024
 N = 1024
 BLOCK = 128
 BANK = 512
-QUAD = 4
 PAIR = 2
 
 FLOPS = 2 * A * S * N * 2 + 2 * A * N
@@ -27,7 +26,7 @@ def tile_isdahead_kernel(tc, w, cov_s, mean_s, feat, y, offs, out):
     class_halves = [slice(0, S // 2), slice(S // 2, S)]
     with (
         tc.tile_pool(name="held", bufs=1) as held,
-        tc.tile_pool(name="logits", bufs=len(halves) * n_blocks // QUAD) as logits,
+        tc.tile_pool(name="logits", bufs=n_blocks // PAIR) as logits,
         tc.tile_pool(name="results", bufs=len(halves) * n_blocks // PAIR) as results,
         tc.psum_pool(name="banks", bufs=8) as banks,
     ):
@@ -45,12 +44,11 @@ def tile_isdahead_kernel(tc, w, cov_s, mean_s, feat, y, offs, out):
                 nc.sync.dma_start(w_t[:], w)
         y_by_block = y.rearrange("(c k) j -> k c j", k=BLOCK)
         out_by_block = out.rearrange("(c k) j -> k c j", k=BLOCK)
-        y_quads = []
-        for samples in halves:
-            for g in range(n_blocks // QUAD):
-                y_quad = logits.tile([BLOCK, QUAD, BANK], F32)
-                nc.sync.dma_start(y_quad[:], y_by_block[:, g * QUAD : (g + 1) * QUAD, samples])
-                y_quads.append(y_quad)
+        y_pairs = []
+        for g in range(n_blocks // PAIR):
+            y_pair = logits.tile([BLOCK, PAIR, N], F32)
+            nc.sync.dma_start(y_pair[:], y_by_block[:, g * PAIR : (g + 1) * PAIR, :])
+            y_pairs.append(y_pair)
 
         quarter = held.tile([A, BLOCK], BF16)
         w_sq_quarter = held.tile([A, S], BF16)
@@ -104,7 +102,7 @@ def tile_isdahead_kernel(tc, w, cov_s, mean_s, feat, y, offs, out):
         for h, samples in enumerate(halves):
             for c in range(n_blocks):
                 classes = slice(c * BLOCK, (c + 1) * BLOCK)
-                y_piece = y_quads[h * (n_blocks // QUAD) + c // QUAD][:, c % QUAD, :]
+                y_piece = y_pairs[c // PAIR][:, c % PAIR, samples]
                 acc = banks.tile([BLOCK, BANK], F32)
                 nc.tensor.matmul(acc[:], w_sq_quarter[:, classes], covn_bf[:, samples], start=True, stop=False)
                 nc.tensor.matmul(acc[:], w_neg_half[:, classes], p_bf[:, samples], start=False, stop=False)

@@ -15,6 +15,7 @@ N = 1024
 BLOCK = 128
 BANK = 512
 PAIR = 2
+STORES = [[2, 2, 2, 2], [2, 2, 2, 1, 1]]
 
 FLOPS = 2 * A * S * N * 2 + 2 * A * N
 
@@ -27,7 +28,7 @@ def tile_isdahead_kernel(tc, w, cov_s, mean_s, feat, y, offs, out):
     with (
         tc.tile_pool(name="held", bufs=1) as held,
         tc.tile_pool(name="logits", bufs=n_blocks // PAIR) as logits,
-        tc.tile_pool(name="results", bufs=len(halves) * n_blocks // PAIR) as results,
+        tc.tile_pool(name="results", bufs=len(STORES[0]) + len(STORES[1])) as results,
         tc.psum_pool(name="banks", bufs=8) as banks,
     ):
         offsets = held.tile([A, N // 16], U16, name="offsets")
@@ -100,15 +101,17 @@ def tile_isdahead_kernel(tc, w, cov_s, mean_s, feat, y, offs, out):
         looked_up_product(1, q, q_bf, p)
 
         for h, samples in enumerate(halves):
-            for c in range(n_blocks):
-                classes = slice(c * BLOCK, (c + 1) * BLOCK)
-                y_piece = y_pairs[c // PAIR][:, c % PAIR, samples]
-                acc = banks.tile([BLOCK, BANK], F32)
-                nc.tensor.matmul(acc[:], w_sq_quarter[:, classes], covn_bf[:, samples], start=True, stop=False)
-                nc.tensor.matmul(acc[:], w_neg_half[:, classes], p_bf[:, samples], start=False, stop=False)
-                nc.tensor.matmul(acc[:], quarter[:], q_bf[:, samples], start=False, stop=True)
-                if c % PAIR == 0:
-                    res = results.tile([BLOCK, PAIR, BANK], F32, name="res")
-                nc.vector.tensor_tensor(res[:, c % PAIR, :], acc[:], y_piece, ADD)
-                if c % PAIR == PAIR - 1:
-                    nc.sync.dma_start(out_by_block[:, c + 1 - PAIR : c + 1, samples], res[:])
+            first = 0
+            for n_in_store in STORES[h]:
+                res = results.tile([BLOCK, n_in_store, BANK], F32, name="res")
+                for i in range(n_in_store):
+                    c = first + i
+                    classes = slice(c * BLOCK, (c + 1) * BLOCK)
+                    y_piece = y_pairs[c // PAIR][:, c % PAIR, samples]
+                    acc = banks.tile([BLOCK, BANK], F32)
+                    nc.tensor.matmul(acc[:], w_sq_quarter[:, classes], covn_bf[:, samples], start=True, stop=False)
+                    nc.tensor.matmul(acc[:], w_neg_half[:, classes], p_bf[:, samples], start=False, stop=False)
+                    nc.tensor.matmul(acc[:], quarter[:], q_bf[:, samples], start=False, stop=True)
+                    nc.vector.tensor_tensor(res[:, i, :], acc[:], y_piece, ADD)
+                nc.sync.dma_start(out_by_block[:, first : first + n_in_store, samples], res[:])
+                first += n_in_store

@@ -14,6 +14,7 @@ S = 1024
 N = 1024
 BLOCK = 128
 BANK = 512
+PIECE = 256
 PAIR = 2
 STORES = [[2, 2, 2, 2], [2, 2, 2, 1, 1]]
 
@@ -63,42 +64,42 @@ def tile_isdahead_kernel(tc, w, cov_s, mean_s, feat, y, offs, out):
         diff_sq = held.tile([A, N], F32)
         covn = held.tile([A, N], F32)
         p = held.tile([A, N], F32)
-        q = held.tile([A, N], F32)
+        q_second = held.tile([A, BANK], F32)
+        q_halves = [mean_t[:, halves[1]], q_second[:]]
+        p_halves = [p[:, samples] for samples in halves]
+        covn_halves = [covn[:, samples] for samples in halves]
         covn_bf = held.tile([A, N], BF16)
         p_bf = held.tile([A, N], BF16)
         q_bf = held.tile([A, N], BF16)
 
-        def squared_difference(h):
-            samples = halves[h]
+        def squared_difference(samples):
             nc.vector.tensor_tensor(diff[:, samples], mean_t[:, samples], feat_t[:, samples], SUBTRACT)
             nc.scalar.activation(diff_sq[:, samples], diff[:, samples], SQUARE, scale=0.5)
 
-        def covariance(h):
-            samples = halves[h]
+        def covariance(samples):
             nc.vector.scalar_tensor_tensor(covn[:, samples], cov_t[:, samples], 0.5, diff_sq[:, samples], MULT, ADD)
-            if h == 0:
-                nc.vector.tensor_copy(covn_bf[:, samples], covn[:, samples])
-            else:
-                nc.scalar.copy(covn_bf[:, samples], covn[:, samples])
+            nc.scalar.copy(covn_bf[:, samples], covn[:, samples])
 
         def looked_up_product(h, product, product_bf, factor):
-            samples = halves[h]
             piece = offsets[:, h * (BANK // 16) : (h + 1) * (BANK // 16)]
-            nc.vector.tensor_tensor(product[:, samples], w_t[:].indirect(piece), factor[:, samples], MULT)
-            nc.scalar.copy(product_bf[:, samples], product[:, samples])
+            nc.vector.tensor_tensor(product[h], w_t[:].indirect(piece), factor[h], MULT)
+            nc.scalar.copy(product_bf[:, halves[h]], product[h])
 
-        squared_difference(0)
-        covariance(0)
+        first_pieces = [slice(j, j + PIECE) for j in range(0, BANK, PIECE)]
+        for piece in first_pieces:
+            squared_difference(piece)
+        for piece in first_pieces:
+            covariance(piece)
         nc.scalar.activation(w_sq_quarter[:, class_halves[0]], w_t[:, class_halves[0]], SQUARE, scale=0.5)
         nc.scalar.activation(w_sq_quarter[:, class_halves[1]], w_t[:, class_halves[1]], SQUARE, scale=0.5)
         nc.scalar.activation(w_neg_half[:, class_halves[0]], w_t[:, class_halves[0]], COPY, scale=-0.5)
-        looked_up_product(0, p, p_bf, covn)
-        squared_difference(1)
+        looked_up_product(0, p_halves, p_bf, covn_halves)
+        squared_difference(halves[1])
         nc.scalar.activation(w_neg_half[:, class_halves[1]], w_t[:, class_halves[1]], COPY, scale=-0.5)
-        looked_up_product(0, q, q_bf, p)
-        covariance(1)
-        looked_up_product(1, p, p_bf, covn)
-        looked_up_product(1, q, q_bf, p)
+        looked_up_product(0, q_halves, q_bf, p_halves)
+        covariance(halves[1])
+        looked_up_product(1, p_halves, p_bf, covn_halves)
+        looked_up_product(1, q_halves, q_bf, p_halves)
 
         for h, samples in enumerate(halves):
             first = 0

@@ -15,7 +15,7 @@ N = 1024
 BLOCK = 128
 BANK = 512
 PIECE = 256
-PAIR = 2
+Y_LOADS = [4, 2, 2]
 STORES = [[2, 2, 2, 2], [2, 2, 2, 1, 1]]
 
 FLOPS = 2 * A * S * N * 2 + 2 * A * N
@@ -25,10 +25,9 @@ def tile_isdahead_kernel(tc, w, cov_s, mean_s, feat, y, offs, out):
     nc = tc.nc
     n_blocks = S // BLOCK
     halves = [slice(h * BANK, (h + 1) * BANK) for h in range(N // BANK)]
-    class_halves = [slice(0, S // 2), slice(S // 2, S)]
     with (
         tc.tile_pool(name="held", bufs=1) as held,
-        tc.tile_pool(name="logits", bufs=n_blocks // PAIR) as logits,
+        tc.tile_pool(name="logits", bufs=len(Y_LOADS)) as logits,
         tc.tile_pool(name="results", bufs=len(STORES[0]) + len(STORES[1])) as results,
         tc.psum_pool(name="banks", bufs=8) as banks,
     ):
@@ -44,13 +43,14 @@ def tile_isdahead_kernel(tc, w, cov_s, mean_s, feat, y, offs, out):
             nc.sync.dma_start(cov_t[:, samples], cov_s[:, samples])
             if h == 0:
                 nc.sync.dma_start(w_t[:], w)
-        y_by_block = y.rearrange("(c k) j -> k c j", k=BLOCK)
-        out_by_block = out.rearrange("(c k) j -> k c j", k=BLOCK)
-        y_pairs = []
-        for g in range(n_blocks // PAIR):
-            y_pair = logits.tile([BLOCK, PAIR, N], F32)
-            nc.sync.dma_start(y_pair[:], y_by_block[:, g * PAIR : (g + 1) * PAIR, :])
-            y_pairs.append(y_pair)
+        y_by_block = y.rearrange("(k c) j -> k c j", k=BLOCK)
+        out_by_block = out.rearrange("(k c) j -> k c j", k=BLOCK)
+        y_blocks = []
+        for n_in_load in Y_LOADS:
+            first = len(y_blocks)
+            y_load = logits.tile([BLOCK, n_in_load, N], F32)
+            nc.sync.dma_start(y_load[:], y_by_block[:, first : first + n_in_load, :])
+            y_blocks.extend([y_load[:, i, :] for i in range(n_in_load)])
 
         quarter = held.tile([A, BLOCK], BF16)
         w_sq_quarter = held.tile([A, S], BF16)
@@ -78,7 +78,6 @@ def tile_isdahead_kernel(tc, w, cov_s, mean_s, feat, y, offs, out):
 
         def covariance(samples):
             nc.vector.scalar_tensor_tensor(covn[:, samples], cov_t[:, samples], 0.5, diff_sq[:, samples], MULT, ADD)
-            nc.scalar.copy(covn_bf[:, samples], covn[:, samples])
 
         def looked_up_product(h, product, product_bf, factor):
             piece = offsets[:, h * (BANK // 16) : (h + 1) * (BANK // 16)]
@@ -90,14 +89,15 @@ def tile_isdahead_kernel(tc, w, cov_s, mean_s, feat, y, offs, out):
             squared_difference(piece)
         for piece in first_pieces:
             covariance(piece)
-        nc.scalar.activation(w_sq_quarter[:, class_halves[0]], w_t[:, class_halves[0]], SQUARE, scale=0.5)
-        nc.scalar.activation(w_sq_quarter[:, class_halves[1]], w_t[:, class_halves[1]], SQUARE, scale=0.5)
-        nc.scalar.activation(w_neg_half[:, class_halves[0]], w_t[:, class_halves[0]], COPY, scale=-0.5)
+        for piece in first_pieces:
+            nc.vector.tensor_copy(covn_bf[:, piece], covn[:, piece])
+        nc.scalar.activation(w_sq_quarter[:], w_t[:], SQUARE, scale=0.5)
+        nc.scalar.activation(w_neg_half[:], w_t[:], COPY, scale=-0.5)
         looked_up_product(0, p_halves, p_bf, covn_halves)
         squared_difference(halves[1])
-        nc.scalar.activation(w_neg_half[:, class_halves[1]], w_t[:, class_halves[1]], COPY, scale=-0.5)
         looked_up_product(0, q_halves, q_bf, p_halves)
         covariance(halves[1])
+        nc.scalar.copy(covn_bf[:, halves[1]], covn[:, halves[1]])
         looked_up_product(1, p_halves, p_bf, covn_halves)
         looked_up_product(1, q_halves, q_bf, p_halves)
 
@@ -107,12 +107,11 @@ def tile_isdahead_kernel(tc, w, cov_s, mean_s, feat, y, offs, out):
                 res = results.tile([BLOCK, n_in_store, BANK], F32, name="res")
                 for i in range(n_in_store):
                     c = first + i
-                    classes = slice(c * BLOCK, (c + 1) * BLOCK)
-                    y_piece = y_pairs[c // PAIR][:, c % PAIR, samples]
+                    classes = slice(c, S, n_blocks)
                     acc = banks.tile([BLOCK, BANK], F32)
                     nc.tensor.matmul(acc[:], w_sq_quarter[:, classes], covn_bf[:, samples], start=True, stop=False)
                     nc.tensor.matmul(acc[:], w_neg_half[:, classes], p_bf[:, samples], start=False, stop=False)
                     nc.tensor.matmul(acc[:], quarter[:], q_bf[:, samples], start=False, stop=True)
-                    nc.vector.tensor_tensor(res[:, i, :], acc[:], y_piece, ADD)
+                    nc.vector.tensor_tensor(res[:, i, :], acc[:], y_blocks[c][:, samples], ADD)
                 nc.sync.dma_start(out_by_block[:, first : first + n_in_store, samples], res[:])
                 first += n_in_store

@@ -80,8 +80,11 @@ def tile_isdahead_kernel(tc, w, cov_s, mean_s, feat, y, offs, out):
             nc.vector.scalar_tensor_tensor(covn[:, samples], cov_t[:, samples], 0.5, diff_sq[:, samples], MULT, ADD)
 
         def looked_up_product(h, product, product_bf, factor):
-            piece = offsets[:, h * (BANK // 16) : (h + 1) * (BANK // 16)]
-            nc.vector.tensor_tensor(product[h], w_t[:].indirect(piece), factor[h], MULT)
+            for j in range(0, BANK, PIECE):
+                piece = slice(j, j + PIECE)
+                entry = (h * BANK + j) // 16
+                entries = offsets[:, entry : entry + PIECE // 16]
+                nc.vector.tensor_tensor(product[h][:, piece], w_t[:].indirect(entries), factor[h][:, piece], MULT)
             nc.scalar.copy(product_bf[:, halves[h]], product[h])
 
         first_pieces = [slice(j, j + PIECE) for j in range(0, BANK, PIECE)]

import concourse.mybir as mybir

F32 = mybir.dt.float32
BF16 = mybir.dt.bfloat16
U16 = mybir.dt.uint16
ADD = mybir.AluOpType.add
SUBTRACT = mybir.AluOpType.subtract
MULT = mybir.AluOpType.mult
COPY = mybir.ActivationFunctionType.Copy
SQUARE = mybir.ActivationFunctionType.Square

A = 128
S = 1024
N = 1024
BLOCK = 128
BANK = 512
PIECE = 256
Y_LOADS = [4, 2, 2]
STORES = [[2, 2, 2, 2], [2, 2, 2, 1, 1]]

FLOPS = 2 * A * S * N * 2 + 2 * A * N


def tile_isdahead_kernel(tc, w, cov_s, mean_s, feat, y, offs, out):
    nc = tc.nc
    n_blocks = S // BLOCK
    halves = [slice(h * BANK, (h + 1) * BANK) for h in range(N // BANK)]
    with (
        tc.tile_pool(name="held", bufs=1) as held,
        tc.tile_pool(name="logits", bufs=len(Y_LOADS)) as logits,
        tc.tile_pool(name="results", bufs=len(STORES[0]) + len(STORES[1])) as results,
        tc.psum_pool(name="banks", bufs=8) as banks,
    ):
        offsets = held.tile([A, N // 16], U16, name="offsets")
        nc.sync.dma_start(offsets[:], offs)
        mean_t = held.tile([A, N], F32)
        feat_t = held.tile([A, N], F32)
        cov_t = held.tile([A, N], F32)
        w_t = held.tile([A, S], F32)
        for h, samples in enumerate(halves):
            nc.sync.dma_start(mean_t[:, samples], mean_s[:, samples])
            nc.sync.dma_start(feat_t[:, samples], feat[:, samples])
            nc.sync.dma_start(cov_t[:, samples], cov_s[:, samples])
            if h == 0:
                nc.sync.dma_start(w_t[:], w)
        y_by_block = y.rearrange("(k c) j -> k c j", k=BLOCK)
        out_by_block = out.rearrange("(k c) j -> k c j", k=BLOCK)
        y_blocks = []
        for n_in_load in Y_LOADS:
            first = len(y_blocks)
            y_load = logits.tile([BLOCK, n_in_load, N], F32)
            nc.sync.dma_start(y_load[:], y_by_block[:, first : first + n_in_load, :])
            y_blocks.extend([y_load[:, i, :] for i in range(n_in_load)])

        quarter = held.tile([A, BLOCK], BF16)
        w_sq_quarter = held.tile([A, S], BF16)
        w_neg_half = held.tile([A, S], BF16)

        half = held.tile([A, BLOCK], BF16)
        nc.vector.memset(half[:], 0.5)
        nc.scalar.activation(quarter[:], half[:], SQUARE)

        diff = held.tile([A, N], F32)
        diff_sq = held.tile([A, N], F32)
        covn = held.tile([A, N], F32)
        p = held.tile([A, N], F32)
        q_second = held.tile([A, BANK], F32)
        q_halves = [mean_t[:, halves[1]], q_second[:]]
        p_halves = [p[:, samples] for samples in halves]
        covn_halves = [covn[:, samples] for samples in halves]
        covn_bf = held.tile([A, N], BF16)
        p_bf = held.tile([A, N], BF16)
        q_bf = held.tile([A, N], BF16)

        def squared_difference(samples):
            nc.vector.tensor_tensor(diff[:, samples], mean_t[:, samples], feat_t[:, samples], SUBTRACT)
            nc.scalar.activation(diff_sq[:, samples], diff[:, samples], SQUARE, scale=0.5)

        def covariance(samples):
            nc.vector.scalar_tensor_tensor(covn[:, samples], cov_t[:, samples], 0.5, diff_sq[:, samples], MULT, ADD)

        def looked_up_product(h, product, product_bf, factor):
            for j in range(0, BANK, PIECE):
                piece = slice(j, j + PIECE)
                entry = (h * BANK + j) // 16
                entries = offsets[:, entry : entry + PIECE // 16]
                nc.vector.tensor_tensor(product[h][:, piece], w_t[:].indirect(entries), factor[h][:, piece], MULT)
            nc.scalar.copy(product_bf[:, halves[h]], product[h])

        first_pieces = [slice(j, j + PIECE) for j in range(0, BANK, PIECE)]
        for piece in first_pieces:
            squared_difference(piece)
        for piece in first_pieces:
            covariance(piece)
        for piece in first_pieces:
            nc.vector.tensor_copy(covn_bf[:, piece], covn[:, piece])
        nc.scalar.activation(w_sq_quarter[:], w_t[:], SQUARE, scale=0.5)
        nc.scalar.activation(w_neg_half[:], w_t[:], COPY, scale=-0.5)
        looked_up_product(0, p_halves, p_bf, covn_halves)
        squared_difference(halves[1])
        looked_up_product(0, q_halves, q_bf, p_halves)
        covariance(halves[1])
        nc.scalar.copy(covn_bf[:, halves[1]], covn[:, halves[1]])
        looked_up_product(1, p_halves, p_bf, covn_halves)
        looked_up_product(1, q_halves, q_bf, p_halves)

        for h, samples in enumerate(halves):
            first = 0
            for n_in_store in STORES[h]:
                res = results.tile([BLOCK, n_in_store, BANK], F32, name="res")
                for i in range(n_in_store):
                    c = first + i
                    classes = slice(c, S, n_blocks)
                    acc = banks.tile([BLOCK, BANK], F32)
                    nc.tensor.matmul(acc[:], w_sq_quarter[:, classes], covn_bf[:, samples], start=True, stop=False)
                    nc.tensor.matmul(acc[:], w_neg_half[:, classes], p_bf[:, samples], start=False, stop=False)
                    nc.tensor.matmul(acc[:], quarter[:], q_bf[:, samples], start=False, stop=True)
                    nc.vector.tensor_tensor(res[:, i, :], acc[:], y_blocks[c][:, samples], ADD)
                nc.sync.dma_start(out_by_block[:, first : first + n_in_store, samples], res[:])
                first += n_in_store
